import numpy as np
import ml_dtypes


def mxq(x, axis, fmt="e4m3"):
    dtype, down = {"e4m3": (ml_dtypes.float8_e4m3fn, 7), "e5m2": (ml_dtypes.float8_e5m2, 14)}[fmt]
    v = np.moveaxis(np.asarray(x, np.float32).astype(ml_dtypes.bfloat16).astype(np.float64), axis, -1)
    blocks = v.reshape(v.shape[:-1] + (-1, 32))
    amax = np.abs(blocks).max(-1, keepdims=True)
    byte = np.maximum(np.where(amax > 0, np.frexp(amax)[1] - 1 + 127, 0) - down, 1)
    scale = np.exp2(byte - 127.0)
    codes = (blocks / scale).astype(np.float32).astype(dtype).astype(np.float64)
    return np.moveaxis((codes * scale).reshape(v.shape), -1, axis)


WIDE = False


def mx_kscale(k):
    if not WIDE:
        return np.ones(k)
    levels = np.array([10, -10, 5, -5, 0])
    a = np.random.permutation(np.resize(levels, k // 512 * 4)).reshape(k // 512, 4)
    idx = np.arange(k)
    return np.exp2(a[idx // 512, idx % 128 // 32])


BF16 = ml_dtypes.bfloat16


def bf(x):
    return np.asarray(x, np.float32).astype(BF16)


def f64(x):
    return np.asarray(x).astype(np.float64)


E, D_COMM, D_REL, D_HET, D_HID = 2048, 2048, 1024, 128, 1024
D_IN = D_COMM + D_REL


def setup_inputs():
    s, t = mx_kscale(D_REL), mx_kscale(D_HID)
    spread = np.exp(0.5 * np.random.standard_normal((E, 1)))
    return {"Mij": bf(np.random.standard_normal((E, D_REL)) * s),
            "f_weights": bf(np.random.standard_normal((E, D_HET)) * np.sqrt(2.0 / D_HET) * spread),
            "W1_rel": bf(np.random.standard_normal((D_REL, D_HID)) / np.sqrt(D_IN) / s[:, None] * t),
            "node_bias": bf(np.random.standard_normal(D_HID) * np.sqrt(D_COMM / D_IN) * t),
            "W2": bf(np.random.standard_normal((D_HID, D_HET)) / np.sqrt(D_HID) / t[:, None]),
            "b2": bf(np.random.standard_normal(D_HET) * 0.1)}


def reference(Mij, f_weights, W1_rel, node_bias, W2, b2):
    h = np.maximum((mxq(f64(Mij), 1, "e4m3") @ mxq(f64(W1_rel), 0, "e4m3")) + f64(node_bias), 0.0)
    out = (mxq(h, 1, "e4m3") @ mxq(f64(W2), 0, "e4m3")) + f64(b2)
    msg = out * f64(f_weights)
    norm = np.sqrt((msg * msg).sum(axis=1, keepdims=True))
    scale = np.where(norm > 1.0, 1.0 / np.maximum(norm, 1.0), 1.0)
    return msg * scale

@@ -1,0 +1,270 @@
+from contextlib import ExitStack
+
+import concourse.mybir as mybir
+from concourse.masks import make_identity
+
+F32 = mybir.dt.float32
+BF16 = mybir.dt.bfloat16
+U32 = mybir.dt.uint32
+U8 = mybir.dt.uint8
+FP8X4 = mybir.dt.float8_e4m3fn_x4
+ACT = mybir.ActivationFunctionType
+ALU = mybir.AluOpType
+
+P = 128
+PACK = 4
+PASSES = 2
+EDGES, D_REL, D_HID, D_HET = 2048, 1024, 1024, 128
+BLOCK = 512
+N_BLOCKS = EDGES // BLOCK
+TILES = BLOCK // P
+HID_TILES = D_HID // P
+N_ROUNDS = N_BLOCKS * PASSES
+N_PAIRS = N_BLOCKS * 2
+PAIRS_AHEAD = 3
+RUN = 4
+
+FLOPS = 2 * EDGES * D_REL * D_HID + 2 * EDGES * D_HID * D_HET
+
+
+def tile_filter_pa_kernel(tc, Mij, f_weights, W1_rel, node_bias, W2, b2, out):
+    nc = tc.nc
+
+    mij_view = Mij.rearrange("(b p t) k -> b p t k", b=N_BLOCKS, p=P, t=TILES)
+    fw_view = f_weights.rearrange("(b p t) h -> p b t h", b=N_BLOCKS, p=P, t=TILES)
+    out_view = out.rearrange("(b p t) h -> b p t h", b=N_BLOCKS, p=P, t=TILES)
+    w1_view = W1_rel.rearrange("(g u p e) n -> g p u e n", g=PASSES, u=2, p=P, e=2)
+    w2_view = W2.rearrange("(g t p) n -> p g t n", g=PASSES, t=PACK, p=P)
+    nb_view = node_bias.rearrange("(r c) -> r c", c=P)
+
+    with ExitStack() as ctx:
+        ctx.enter_context(tc.manual_schedule())
+        const = ctx.enter_context(tc.tile_pool(name="const", bufs=1))
+        stage = ctx.enter_context(tc.tile_pool(name="stage", bufs=2))
+        psum_tr = ctx.enter_context(tc.psum_pool(name="psum_tr", bufs=2))
+        psum_h = ctx.enter_context(tc.psum_pool(name="psum_h", bufs=4))
+        psum_o = ctx.enter_context(tc.psum_pool(name="psum_o", bufs=2))
+
+        mij_raw = [
+            const.tile([P, TILES, D_REL], BF16, name="mij_raw%d" % b) for b in range(N_BLOCKS)
+        ]
+        w1_raw = const.tile([P, PASSES, 2, 2, D_HID], BF16)
+        nb_rows = const.tile([P, P], BF16)
+        nc.vector.memset(nb_rows[:], 0.0)
+        nc.sync.dma_start(out=nb_rows[0:HID_TILES, :], in_=nb_view)
+        nc.sync.dma_start(out=mij_raw[0][:], in_=mij_view[0])
+        for g in range(PASSES):
+            nc.sync.dma_start(out=w1_raw[:, g], in_=w1_view[g])
+        for b in range(1, N_BLOCKS):
+            nc.sync.dma_start(out=mij_raw[b][:], in_=mij_view[b])
+
+        w2_raw = const.tile([P, PASSES, PACK, D_HET], BF16)
+        nc.scalar.dma_start(out=w2_raw[:], in_=w2_view)
+        b2_all = const.tile([P, D_HET], BF16)
+        nc.scalar.dma_start(out=b2_all[:], in_=b2.partition_broadcast(P))
+        fw_sb = const.tile([P, N_BLOCKS, TILES, D_HET], BF16)
+        nc.scalar.dma_start(out=fw_sb[:], in_=fw_view)
+
+        ident = const.tile([P, P], F32)
+        make_identity(nc, ident[:])
+        plus_one = const.tile([P, 1], F32)
+        nc.vector.memset(plus_one[:], 1.0)
+        minus_one = const.tile([P, 1], F32)
+        nc.vector.memset(minus_one[:], -1.0)
+        warm = const.tile([P, 1], F32)
+        nc.scalar.activation(out=warm[:], in_=plus_one[:], func=ACT.Sqrt)
+
+        nb_f32 = const.tile([P, P], F32)
+        nc.vector.tensor_copy(out=nb_f32[:], in_=nb_rows[:])
+        nb_col = const.tile([P, HID_TILES], F32)
+
+        w1_codes = const.tile([P, PASSES, D_HID], U32, align_bytes=64)
+        w1_scales = const.tile([P, PASSES, D_HID], U8, align_bytes=64)
+        w2_codes = const.tile([P, PASSES, D_HET], U32, align_bytes=64)
+        w2_scales = const.tile([P, PASSES, D_HET], U8, align_bytes=64)
+        mij_grp, mij_codes, mij_scales = {}, {}, {}
+        h_planes, h_grp, h_codes, h_scales = {}, {}, {}, {}
+        o_bank, msg, factor = {}, {}, {}
+
+        def regroup(dst, src):
+            nc.vector.tensor_copy(
+                out=dst.rearrange("p (c i) j -> p c j i", i=RUN),
+                in_=src.rearrange("p j (c i) -> p c j i", i=RUN),
+            )
+
+        def quantise(codes, scales, grouped):
+            nc.vector.quantize_mx(out=codes.bitcast(FP8X4), scales=scales, in_=grouped)
+
+        def transpose_pair(pair):
+            b, half = divmod(pair, 2)
+            if half == 0:
+                mij_grp[b] = stage.tile([P, PASSES, BLOCK, 2], F32, name="mij_grp", tag="mij_grp", align_bytes=64)
+            for t in (2 * half, 2 * half + 1):
+                words = mij_raw[b][:, t, :].bitcast(F32)
+                bank = psum_tr.tile([P, PASSES, 2, P], F32, name="tr_bank", tag="tr")
+                for g in range(PASSES):
+                    for u in range(2):
+                        first = (2 * g + u) * P
+                        nc.tensor.transpose(bank[:, g, u, :], words[:, first : first + P], ident[:])
+                nc.scalar.copy(
+                    out=mij_grp[b][:, :, t * P : (t + 1) * P, :],
+                    in_=bank[:].rearrange("p g u e -> p g e u"),
+                )
+
+        def quantise_mij(b):
+            mij_codes[b] = stage.tile([P, PASSES, BLOCK], U32, name="mij_codes", tag="mij_codes", align_bytes=64)
+            mij_scales[b] = stage.tile([P, PASSES, BLOCK], U8, name="mij_scales", tag="mij_scales", align_bytes=64)
+            quantise(
+                mij_codes[b][:].rearrange("p g e -> p (g e)"),
+                mij_scales[b][:].rearrange("p g e -> p (g e)"),
+                mij_grp[b][:].rearrange("p g e u -> p (g e u)").bitcast(BF16),
+            )
+
+        w1_grp = {}
+
+        def regroup_w1(g, half):
+            cols = slice(half * BLOCK, (half + 1) * BLOCK)
+            w1_grp[(g, half)] = stage.tile([P, BLOCK, PACK], BF16, name="w1_grp", tag="w1_grp", align_bytes=64)
+            regroup(w1_grp[(g, half)][:], w1_raw[:, g].rearrange("p u e n -> p (u e) n")[:, :, cols])
+
+        def quantise_w1(g, half):
+            cols = slice(half * BLOCK, (half + 1) * BLOCK)
+            quantise(
+                w1_codes[:, g, cols], w1_scales[:, g, cols], w1_grp[(g, half)][:].rearrange("p n j -> p (n j)")
+            )
+
+        def first_layer(b, m):
+            g2, t = divmod(m, PACK)
+            if t == 0:
+                h_planes[(b, g2)] = stage.tile([P, PACK, BLOCK], BF16, name="h_planes", tag="h_planes")
+            cols = slice(m * P, (m + 1) * P)
+            bank = psum_h.tile([P, BLOCK], F32, name="h_bank", tag="h")
+            for g in range(PASSES):
+                nc.tensor.matmul_mx(
+                    out=bank[:],
+                    lhsT=w1_codes[:, g, cols].bitcast(FP8X4),
+                    lhsT_scale=w1_scales[:, g, cols],
+                    rhs=mij_codes[b][:, g, :].bitcast(FP8X4),
+                    rhs_scale=mij_scales[b][:, g, :],
+                    start=(g == 0),
+                    stop=(g == PASSES - 1),
+                )
+            nc.scalar.activation(
+                out=h_planes[(b, g2)][:, t, :], in_=bank[:], func=ACT.Relu, bias=nb_col[:, m : m + 1], scale=1.0
+            )
+
+        def regroup_h(b, g2):
+            h_grp[(b, g2)] = stage.tile([P, BLOCK, PACK], BF16, name="h_grp", tag="h_grp", align_bytes=64)
+            regroup(h_grp[(b, g2)][:], h_planes[(b, g2)][:])
+
+        def quantise_h(b, g2):
+            if g2 == 0:
+                h_codes[b] = stage.tile([P, PASSES, BLOCK], U32, name="h_codes", tag="h_codes", align_bytes=64)
+                h_scales[b] = stage.tile([P, PASSES, BLOCK], U8, name="h_scales", tag="h_scales", align_bytes=64)
+            quantise(h_codes[b][:, g2, :], h_scales[b][:, g2, :], h_grp[(b, g2)][:].rearrange("p e j -> p (e j)"))
+
+        def second_layer(b):
+            o_bank[b] = psum_o.tile([P, TILES, D_HET], F32, name="o_bank", tag="o")
+            for t in range(TILES):
+                cols = slice(t * P, (t + 1) * P)
+                for g2 in range(PASSES):
+                    nc.tensor.matmul_mx(
+                        out=o_bank[b][:, t, :],
+                        lhsT=h_codes[b][:, g2, cols].bitcast(FP8X4),
+                        lhsT_scale=h_scales[b][:, g2, cols],
+                        rhs=w2_codes[:, g2, :].bitcast(FP8X4),
+                        rhs_scale=w2_scales[:, g2, :],
+                        start=(g2 == 0),
+                        stop=(g2 == PASSES - 1),
+                    )
+
+        def message(b):
+            biased = stage.tile([P, TILES, D_HET], F32, name="biased", tag="biased")
+            nc.vector.tensor_tensor(
+                out=biased[:],
+                in0=o_bank[b][:],
+                in1=b2_all[:].unsqueeze(1).to_broadcast([P, TILES, D_HET]),
+                op=ALU.add,
+            )
+            msg[b] = stage.tile([P, TILES, D_HET], F32, name="msg", tag="msg")
+            nc.vector.tensor_tensor(out=msg[b][:], in0=biased[:], in1=fw_sb[:, b], op=ALU.mult)
+
+        def clamped_norm(b):
+            squares = stage.tile([P, TILES, D_HET], F32, name="squares", tag="squares")
+            sumsq = stage.tile([P, TILES], F32, name="sumsq", tag="sumsq")
+            for t in range(TILES):
+                nc.scalar.activation(
+                    out=squares[:, t, :], in_=msg[b][:, t, :], func=ACT.Square, accum_out=sumsq[:, t : t + 1]
+                )
+            excess = stage.tile([P, TILES], F32, name="excess", tag="excess")
+            nc.scalar.activation(out=excess[:], in_=sumsq[:], func=ACT.Relu, bias=minus_one[:], scale=1.0)
+            factor[b] = stage.tile([P, TILES], F32, name="norm", tag="norm")
+            nc.scalar.activation(out=factor[b][:], in_=excess[:], func=ACT.Sqrt, bias=plus_one[:], scale=1.0)
+
+        def scale_and_store(b):
+            inverse = stage.tile([P, TILES], F32, name="inverse", tag="inverse")
+            nc.vector.reciprocal(out=inverse[:], in_=factor[b][:])
+            result = stage.tile([P, TILES, D_HET], F32, name="result", tag="result")
+            nc.vector.tensor_tensor(
+                out=result[:],
+                in0=msg[b][:],
+                in1=inverse[:].unsqueeze(2).to_broadcast([P, TILES, D_HET]),
+                op=ALU.mult,
+            )
+            nc.sync.dma_start(out=out_view[b], in_=result[:])
+
+        def prepare_w2():
+            w2_grp = const.tile([P, PASSES, D_HET, PACK], BF16, align_bytes=64)
+            for g2 in range(PASSES):
+                regroup(w2_grp[:, g2], w2_raw[:, g2])
+            quantise(
+                w2_codes[:].rearrange("p g n -> p (g n)"),
+                w2_scales[:].rearrange("p g n -> p (g n)"),
+                w2_grp[:].rearrange("p g n j -> p (g n j)"),
+            )
+
+        transpose_pair(0)
+        transpose_pair(1)
+        nb_bank = psum_tr.tile([P, P], F32, name="nb_bank", tag="tr")
+        nc.tensor.transpose(nb_bank[:], nb_f32[:], ident[:])
+        regroup_w1(0, 0)
+        quantise_mij(0)
+        regroup_w1(1, 0)
+        nc.vector.tensor_copy(out=nb_col[:], in_=nb_bank[:, 0:HID_TILES])
+        quantise_w1(0, 0)
+        quantise_w1(1, 0)
+        regroup_w1(0, 1)
+        regroup_w1(1, 1)
+        quantise_w1(0, 1)
+        quantise_w1(1, 1)
+
+        next_pair = 2
+        next_block = 1
+        for r in range(N_ROUNDS):
+            b, g2 = divmod(r, PASSES)
+            for t in range(PACK):
+                first_layer(b, g2 * PACK + t)
+            if g2 == 1 and b >= 1:
+                clamped_norm(b - 1)
+            while next_pair < min(r + PAIRS_AHEAD + 1, N_PAIRS):
+                transpose_pair(next_pair)
+                next_pair += 1
+            if g2 == 0 and b >= 1:
+                second_layer(b - 1)
+            regroup_h(b, g2)
+            if next_block < N_BLOCKS and 2 * (next_block + 1) <= next_pair:
+                quantise_mij(next_block)
+                next_block += 1
+            if g2 == 1 and b >= 1:
+                scale_and_store(b - 1)
+            if r == 1:
+                prepare_w2()
+            quantise_h(b, g2)
+            if g2 == 0 and b >= 1:
+                message(b - 1)
+
+        last = N_BLOCKS - 1
+        second_layer(last)
+        message(last)
+        clamped_norm(last)
+        scale_and_store(last)

@@ -38,7 +38,6 @@ def tile_filter_pa_kernel(tc, Mij, f_weights, W1_rel, node_bias, W2, b2, out):
     nb_view = node_bias.rearrange("(r c) -> r c", c=P)
 
     with ExitStack() as ctx:
-        ctx.enter_context(tc.manual_schedule())
         const = ctx.enter_context(tc.tile_pool(name="const", bufs=1))
         stage = ctx.enter_context(tc.tile_pool(name="stage", bufs=2))
         psum_tr = ctx.enter_context(tc.psum_pool(name="psum_tr", bufs=2))

@@ -19,9 +19,7 @@ BLOCK = 512
 N_BLOCKS = EDGES // BLOCK
 TILES = BLOCK // P
 HID_TILES = D_HID // P
-N_ROUNDS = N_BLOCKS * PASSES
-N_PAIRS = N_BLOCKS * 2
-PAIRS_AHEAD = 3
+BLOCKS_AHEAD = 1
 RUN = 4
 
 FLOPS = 2 * EDGES * D_REL * D_HID + 2 * EDGES * D_HID * D_HET
@@ -39,7 +37,7 @@ def tile_filter_pa_kernel(tc, Mij, f_weights, W1_rel, node_bias, W2, b2, out):
 
     with ExitStack() as ctx:
         const = ctx.enter_context(tc.tile_pool(name="const", bufs=1))
-        stage = ctx.enter_context(tc.tile_pool(name="stage", bufs=2))
+        stage = ctx.enter_context(tc.tile_pool(name="stage", bufs=3))
         psum_tr = ctx.enter_context(tc.psum_pool(name="psum_tr", bufs=2))
         psum_h = ctx.enter_context(tc.psum_pool(name="psum_h", bufs=4))
         psum_o = ctx.enter_context(tc.psum_pool(name="psum_o", bufs=2))
@@ -58,11 +56,11 @@ def tile_filter_pa_kernel(tc, Mij, f_weights, W1_rel, node_bias, W2, b2, out):
             nc.sync.dma_start(out=mij_raw[b][:], in_=mij_view[b])
 
         w2_raw = const.tile([P, PASSES, PACK, D_HET], BF16)
-        nc.scalar.dma_start(out=w2_raw[:], in_=w2_view)
-        b2_all = const.tile([P, D_HET], BF16)
-        nc.scalar.dma_start(out=b2_all[:], in_=b2.partition_broadcast(P))
+        nc.sync.dma_start(out=w2_raw[:], in_=w2_view)
         fw_sb = const.tile([P, N_BLOCKS, TILES, D_HET], BF16)
-        nc.scalar.dma_start(out=fw_sb[:], in_=fw_view)
+        nc.sync.dma_start(out=fw_sb[:], in_=fw_view)
+        b2_all = const.tile([P, D_HET], BF16)
+        nc.sync.dma_start(out=b2_all[:], in_=b2.partition_broadcast(P))
 
         ident = const.tile([P, P], F32)
         make_identity(nc, ident[:])
@@ -222,48 +220,32 @@ def tile_filter_pa_kernel(tc, Mij, f_weights, W1_rel, node_bias, W2, b2, out):
                 w2_grp[:].rearrange("p g n j -> p (g n j)"),
             )
 
-        transpose_pair(0)
-        transpose_pair(1)
+        def prepare_mij(b):
+            transpose_pair(2 * b)
+            transpose_pair(2 * b + 1)
+            quantise_mij(b)
+
         nb_bank = psum_tr.tile([P, P], F32, name="nb_bank", tag="tr")
         nc.tensor.transpose(nb_bank[:], nb_f32[:], ident[:])
-        regroup_w1(0, 0)
-        quantise_mij(0)
-        regroup_w1(1, 0)
         nc.vector.tensor_copy(out=nb_col[:], in_=nb_bank[:, 0:HID_TILES])
-        quantise_w1(0, 0)
-        quantise_w1(1, 0)
-        regroup_w1(0, 1)
-        regroup_w1(1, 1)
-        quantise_w1(0, 1)
-        quantise_w1(1, 1)
-
-        next_pair = 2
-        next_block = 1
-        for r in range(N_ROUNDS):
-            b, g2 = divmod(r, PASSES)
-            for t in range(PACK):
-                first_layer(b, g2 * PACK + t)
-            if g2 == 1 and b >= 1:
-                clamped_norm(b - 1)
-            while next_pair < min(r + PAIRS_AHEAD + 1, N_PAIRS):
-                transpose_pair(next_pair)
-                next_pair += 1
-            if g2 == 0 and b >= 1:
-                second_layer(b - 1)
-            regroup_h(b, g2)
-            if next_block < N_BLOCKS and 2 * (next_block + 1) <= next_pair:
-                quantise_mij(next_block)
-                next_block += 1
-            if g2 == 1 and b >= 1:
-                scale_and_store(b - 1)
-            if r == 1:
-                prepare_w2()
-            quantise_h(b, g2)
-            if g2 == 0 and b >= 1:
-                message(b - 1)
-
-        last = N_BLOCKS - 1
-        second_layer(last)
-        message(last)
-        clamped_norm(last)
-        scale_and_store(last)
+        prepare_mij(0)
+        for half in range(2):
+            for g in range(PASSES):
+                regroup_w1(g, half)
+            for g in range(PASSES):
+                quantise_w1(g, half)
+        prepare_w2()
+        for b in range(1, BLOCKS_AHEAD + 1):
+            prepare_mij(b)
+        for b in range(N_BLOCKS):
+            for g2 in range(PASSES):
+                for t in range(PACK):
+                    first_layer(b, g2 * PACK + t)
+                regroup_h(b, g2)
+                quantise_h(b, g2)
+            if b + BLOCKS_AHEAD + 1 < N_BLOCKS:
+                prepare_mij(b + BLOCKS_AHEAD + 1)
+            second_layer(b)
+            message(b)
+            clamped_norm(b)
+            scale_and_store(b)

@@ -20,6 +20,7 @@ N_BLOCKS = EDGES // BLOCK
 TILES = BLOCK // P
 HID_TILES = D_HID // P
 BLOCKS_AHEAD = 1
+LAST_PARTS = 2
 RUN = 4
 
 FLOPS = 2 * EDGES * D_REL * D_HID + 2 * EDGES * D_HID * D_HET
@@ -81,7 +82,7 @@ def tile_filter_pa_kernel(tc, Mij, f_weights, W1_rel, node_bias, W2, b2, out):
         w2_scales = const.tile([P, PASSES, D_HET], U8, align_bytes=64)
         mij_grp, mij_codes, mij_scales = {}, {}, {}
         h_planes, h_grp, h_codes, h_scales = {}, {}, {}, {}
-        o_bank, msg, factor = {}, {}, {}
+        o_bank, msg, norm = {}, {}, {}
 
         def regroup(dst, src):
             nc.vector.tensor_copy(
@@ -150,23 +151,34 @@ def tile_filter_pa_kernel(tc, Mij, f_weights, W1_rel, node_bias, W2, b2, out):
                 out=h_planes[(b, g2)][:, t, :], in_=bank[:], func=ACT.Relu, bias=nb_col[:, m : m + 1], scale=1.0
             )
 
-        def regroup_h(b, g2):
-            h_grp[(b, g2)] = stage.tile([P, BLOCK, PACK], BF16, name="h_grp", tag="h_grp", align_bytes=64)
-            regroup(h_grp[(b, g2)][:], h_planes[(b, g2)][:])
+        def edge_cols(tiles):
+            return slice(tiles[0] * P, (tiles[-1] + 1) * P)
 
-        def quantise_h(b, g2):
-            if g2 == 0:
+        def regroup_h(b, g2, tiles):
+            if tiles[0] == 0:
+                h_grp[(b, g2)] = stage.tile([P, BLOCK, PACK], BF16, name="h_grp", tag="h_grp", align_bytes=64)
+            cols = edge_cols(tiles)
+            regroup(h_grp[(b, g2)][:, cols, :], h_planes[(b, g2)][:, :, cols])
+
+        def quantise_h(b, g2, tiles):
+            if g2 == 0 and tiles[0] == 0:
                 h_codes[b] = stage.tile([P, PASSES, BLOCK], U32, name="h_codes", tag="h_codes", align_bytes=64)
                 h_scales[b] = stage.tile([P, PASSES, BLOCK], U8, name="h_scales", tag="h_scales", align_bytes=64)
-            quantise(h_codes[b][:, g2, :], h_scales[b][:, g2, :], h_grp[(b, g2)][:].rearrange("p e j -> p (e j)"))
+            cols = edge_cols(tiles)
+            quantise(
+                h_codes[b][:, g2, cols],
+                h_scales[b][:, g2, cols],
+                h_grp[(b, g2)][:, cols, :].rearrange("p e j -> p (e j)"),
+            )
 
-        def second_layer(b):
-            o_bank[b] = psum_o.tile([P, TILES, D_HET], F32, name="o_bank", tag="o")
-            for t in range(TILES):
+        def second_layer(b, tiles):
+            bank = psum_o.tile([P, len(tiles), D_HET], F32, name="o_bank", tag="o")
+            o_bank[(b, tiles[0])] = bank
+            for i, t in enumerate(tiles):
                 cols = slice(t * P, (t + 1) * P)
                 for g2 in range(PASSES):
                     nc.tensor.matmul_mx(
-                        out=o_bank[b][:, t, :],
+                        out=bank[:, i, :],
                         lhsT=h_codes[b][:, g2, cols].bitcast(FP8X4),
                         lhsT_scale=h_scales[b][:, g2, cols],
                         rhs=w2_codes[:, g2, :].bitcast(FP8X4),
@@ -175,40 +187,41 @@ def tile_filter_pa_kernel(tc, Mij, f_weights, W1_rel, node_bias, W2, b2, out):
                         stop=(g2 == PASSES - 1),
                     )
 
-        def message(b):
-            biased = stage.tile([P, TILES, D_HET], F32, name="biased", tag="biased")
+        def message(b, tiles):
+            shape = [P, len(tiles), D_HET]
+            biased = stage.tile(shape, F32, name="biased", tag="biased")
             nc.vector.tensor_tensor(
-                out=biased[:],
-                in0=o_bank[b][:],
-                in1=b2_all[:].unsqueeze(1).to_broadcast([P, TILES, D_HET]),
-                op=ALU.add,
+                out=biased[:], in0=o_bank[(b, tiles[0])][:], in1=b2_all[:].unsqueeze(1).to_broadcast(shape), op=ALU.add
             )
-            msg[b] = stage.tile([P, TILES, D_HET], F32, name="msg", tag="msg")
-            nc.vector.tensor_tensor(out=msg[b][:], in0=biased[:], in1=fw_sb[:, b], op=ALU.mult)
+            msg[(b, tiles[0])] = stage.tile(shape, F32, name="msg", tag="msg")
+            nc.vector.tensor_tensor(
+                out=msg[(b, tiles[0])][:], in0=biased[:], in1=fw_sb[:, b, tiles[0] : tiles[-1] + 1, :], op=ALU.mult
+            )
 
-        def clamped_norm(b):
-            squares = stage.tile([P, TILES, D_HET], F32, name="squares", tag="squares")
-            sumsq = stage.tile([P, TILES], F32, name="sumsq", tag="sumsq")
-            for t in range(TILES):
+        def clamped_norm(b, tiles):
+            squares = stage.tile([P, len(tiles), D_HET], F32, name="squares", tag="squares")
+            sumsq = stage.tile([P, len(tiles)], F32, name="sumsq", tag="sumsq")
+            for i in range(len(tiles)):
                 nc.scalar.activation(
-                    out=squares[:, t, :], in_=msg[b][:, t, :], func=ACT.Square, accum_out=sumsq[:, t : t + 1]
+                    out=squares[:, i, :],
+                    in_=msg[(b, tiles[0])][:, i, :],
+                    func=ACT.Square,
+                    accum_out=sumsq[:, i : i + 1],
                 )
-            excess = stage.tile([P, TILES], F32, name="excess", tag="excess")
+            excess = stage.tile([P, len(tiles)], F32, name="excess", tag="excess")
             nc.scalar.activation(out=excess[:], in_=sumsq[:], func=ACT.Relu, bias=minus_one[:], scale=1.0)
-            factor[b] = stage.tile([P, TILES], F32, name="norm", tag="norm")
-            nc.scalar.activation(out=factor[b][:], in_=excess[:], func=ACT.Sqrt, bias=plus_one[:], scale=1.0)
+            norm[(b, tiles[0])] = stage.tile([P, len(tiles)], F32, name="norm", tag="norm")
+            nc.scalar.activation(out=norm[(b, tiles[0])][:], in_=excess[:], func=ACT.Sqrt, bias=plus_one[:], scale=1.0)
 
-        def scale_and_store(b):
-            inverse = stage.tile([P, TILES], F32, name="inverse", tag="inverse")
-            nc.vector.reciprocal(out=inverse[:], in_=factor[b][:])
-            result = stage.tile([P, TILES, D_HET], F32, name="result", tag="result")
+        def scale_and_store(b, tiles):
+            shape = [P, len(tiles), D_HET]
+            inverse = stage.tile([P, len(tiles)], F32, name="inverse", tag="inverse")
+            nc.vector.reciprocal(out=inverse[:], in_=norm[(b, tiles[0])][:])
+            result = stage.tile(shape, F32, name="result", tag="result")
             nc.vector.tensor_tensor(
-                out=result[:],
-                in0=msg[b][:],
-                in1=inverse[:].unsqueeze(2).to_broadcast([P, TILES, D_HET]),
-                op=ALU.mult,
+                out=result[:], in0=msg[(b, tiles[0])][:], in1=inverse[:].unsqueeze(2).to_broadcast(shape), op=ALU.mult
             )
-            nc.sync.dma_start(out=out_view[b], in_=result[:])
+            nc.sync.dma_start(out=out_view[b][:, tiles[0] : tiles[-1] + 1, :], in_=result[:])
 
         def prepare_w2():
             w2_grp = const.tile([P, PASSES, D_HET, PACK], BF16, align_bytes=64)
@@ -238,14 +251,18 @@ def tile_filter_pa_kernel(tc, Mij, f_weights, W1_rel, node_bias, W2, b2, out):
         for b in range(1, BLOCKS_AHEAD + 1):
             prepare_mij(b)
         for b in range(N_BLOCKS):
+            n_parts = LAST_PARTS if b == N_BLOCKS - 1 else 1
+            size = TILES // n_parts
+            parts = [list(range(i * size, (i + 1) * size)) for i in range(n_parts)]
             for g2 in range(PASSES):
                 for t in range(PACK):
                     first_layer(b, g2 * PACK + t)
-                regroup_h(b, g2)
-                quantise_h(b, g2)
+                for tiles in parts:
+                    regroup_h(b, g2, tiles)
+                for tiles in parts:
+                    quantise_h(b, g2, tiles)
             if b + BLOCKS_AHEAD + 1 < N_BLOCKS:
                 prepare_mij(b + BLOCKS_AHEAD + 1)
-            second_layer(b)
-            message(b)
-            clamped_norm(b)
-            scale_and_store(b)
+            for step in (second_layer, message, clamped_norm, scale_and_store):
+                for tiles in parts:
+                    step(b, tiles)

@@ -39,9 +39,7 @@ def tile_filter_pa_kernel(tc, Mij, f_weights, W1_rel, node_bias, W2, b2, out):
     with ExitStack() as ctx:
         const = ctx.enter_context(tc.tile_pool(name="const", bufs=1))
         stage = ctx.enter_context(tc.tile_pool(name="stage", bufs=3))
-        psum_tr = ctx.enter_context(tc.psum_pool(name="psum_tr", bufs=2))
-        psum_h = ctx.enter_context(tc.psum_pool(name="psum_h", bufs=4))
-        psum_o = ctx.enter_context(tc.psum_pool(name="psum_o", bufs=2))
+        psum = ctx.enter_context(tc.psum_pool(name="psum", bufs=8))
 
         mij_raw = [
             const.tile([P, TILES, D_REL], BF16, name="mij_raw%d" % b) for b in range(N_BLOCKS)
@@ -99,7 +97,7 @@ def tile_filter_pa_kernel(tc, Mij, f_weights, W1_rel, node_bias, W2, b2, out):
                 mij_grp[b] = stage.tile([P, PASSES, BLOCK, 2], F32, name="mij_grp", tag="mij_grp", align_bytes=64)
             for t in (2 * half, 2 * half + 1):
                 words = mij_raw[b][:, t, :].bitcast(F32)
-                bank = psum_tr.tile([P, PASSES, 2, P], F32, name="tr_bank", tag="tr")
+                bank = psum.tile([P, PASSES, 2, P], F32, name="tr_bank", tag="bank")
                 for g in range(PASSES):
                     for u in range(2):
                         first = (2 * g + u) * P
@@ -136,7 +134,7 @@ def tile_filter_pa_kernel(tc, Mij, f_weights, W1_rel, node_bias, W2, b2, out):
             if t == 0:
                 h_planes[(b, g2)] = stage.tile([P, PACK, BLOCK], BF16, name="h_planes", tag="h_planes")
             cols = slice(m * P, (m + 1) * P)
-            bank = psum_h.tile([P, BLOCK], F32, name="h_bank", tag="h")
+            bank = psum.tile([P, BLOCK], F32, name="h_bank", tag="bank")
             for g in range(PASSES):
                 nc.tensor.matmul_mx(
                     out=bank[:],
@@ -172,7 +170,7 @@ def tile_filter_pa_kernel(tc, Mij, f_weights, W1_rel, node_bias, W2, b2, out):
             )
 
         def second_layer(b, tiles):
-            bank = psum_o.tile([P, len(tiles), D_HET], F32, name="o_bank", tag="o")
+            bank = psum.tile([P, len(tiles), D_HET], F32, name="o_bank", tag="bank")
             o_bank[(b, tiles[0])] = bank
             for i, t in enumerate(tiles):
                 cols = slice(t * P, (t + 1) * P)
@@ -238,7 +236,7 @@ def tile_filter_pa_kernel(tc, Mij, f_weights, W1_rel, node_bias, W2, b2, out):
             transpose_pair(2 * b + 1)
             quantise_mij(b)
 
-        nb_bank = psum_tr.tile([P, P], F32, name="nb_bank", tag="tr")
+        nb_bank = psum.tile([P, P], F32, name="nb_bank", tag="bank")
         nc.tensor.transpose(nb_bank[:], nb_f32[:], ident[:])
         nc.vector.tensor_copy(out=nb_col[:], in_=nb_bank[:, 0:HID_TILES])
         prepare_mij(0)

@@ -18,6 +18,7 @@ EDGES, D_REL, D_HID, D_HET = 2048, 1024, 1024, 128
 BLOCK = 512
 N_BLOCKS = EDGES // BLOCK
 TILES = BLOCK // P
+HALF = D_HID // 2
 HID_TILES = D_HID // P
 BLOCKS_AHEAD = 1
 LAST_PARTS = 2
@@ -32,7 +33,7 @@ def tile_filter_pa_kernel(tc, Mij, f_weights, W1_rel, node_bias, W2, b2, out):
     mij_view = Mij.rearrange("(b p t) k -> b p t k", b=N_BLOCKS, p=P, t=TILES)
     fw_view = f_weights.rearrange("(b p t) h -> p b t h", b=N_BLOCKS, p=P, t=TILES)
     out_view = out.rearrange("(b p t) h -> b p t h", b=N_BLOCKS, p=P, t=TILES)
-    w1_view = W1_rel.rearrange("(g u p e) n -> g p u e n", g=PASSES, u=2, p=P, e=2)
+    w1_view = W1_rel.rearrange("(c p e) n -> e p c n", c=2 * PASSES, p=P, e=2)
     w2_view = W2.rearrange("(g t p) n -> p g t n", g=PASSES, t=PACK, p=P)
     nb_view = node_bias.rearrange("(r c) -> r c", c=P)
 
@@ -44,15 +45,27 @@ def tile_filter_pa_kernel(tc, Mij, f_weights, W1_rel, node_bias, W2, b2, out):
         mij_raw = [
             const.tile([P, TILES, D_REL], BF16, name="mij_raw%d" % b) for b in range(N_BLOCKS)
         ]
-        w1_raw = const.tile([P, PASSES, 2, 2, D_HID], BF16)
+        w1_raw = [const.tile([P, PASSES, 2, 2, HALF], BF16, name="w1_raw%d" % half) for half in range(2)]
         nb_rows = const.tile([P, P], BF16)
         nc.vector.memset(nb_rows[:], 0.0)
         nc.sync.dma_start(out=nb_rows[0:HID_TILES, :], in_=nb_view)
-        nc.sync.dma_start(out=mij_raw[0][:], in_=mij_view[0])
-        for g in range(PASSES):
-            nc.sync.dma_start(out=w1_raw[:, g], in_=w1_view[g])
-        for b in range(1, N_BLOCKS):
+        def load_w1(half):
+            for e in range(2):
+                nc.sync.dma_start(
+                    out=w1_raw[half][:, :, :, e, :].rearrange("p g u n -> p (g u) n"),
+                    in_=w1_view[e][:, :, half * HALF : (half + 1) * HALF],
+                )
+
+        def load_mij(b):
             nc.sync.dma_start(out=mij_raw[b][:], in_=mij_view[b])
+
+        with tc.manual_schedule(engines={mybir.EngineType.SP}):
+            load_w1(0)
+            load_mij(0)
+            load_mij(1)
+            load_w1(1)
+            for b in range(2, N_BLOCKS):
+                load_mij(b)
 
         w2_raw = const.tile([P, PASSES, PACK, D_HET], BF16)
         nc.sync.dma_start(out=w2_raw[:], in_=w2_view)
@@ -68,7 +81,7 @@ def tile_filter_pa_kernel(tc, Mij, f_weights, W1_rel, node_bias, W2, b2, out):
         minus_one = const.tile([P, 1], F32)
         nc.vector.memset(minus_one[:], -1.0)
         warm = const.tile([P, 1], F32)
-        nc.scalar.activation(out=warm[:], in_=plus_one[:], func=ACT.Sqrt)
+        nc.scalar.activation(out=warm[:], in_=plus_one[:], func=ACT.Abs_reciprocal_sqrt)
 
         nb_f32 = const.tile([P, P], F32)
         nc.vector.tensor_copy(out=nb_f32[:], in_=nb_rows[:])
@@ -80,7 +93,7 @@ def tile_filter_pa_kernel(tc, Mij, f_weights, W1_rel, node_bias, W2, b2, out):
         w2_scales = const.tile([P, PASSES, D_HET], U8, align_bytes=64)
         mij_grp, mij_codes, mij_scales = {}, {}, {}
         h_planes, h_grp, h_codes, h_scales = {}, {}, {}, {}
-        o_bank, msg, norm = {}, {}, {}
+        o_bank, msg, factor = {}, {}, {}
 
         def regroup(dst, src):
             nc.vector.tensor_copy(
@@ -119,12 +132,11 @@ def tile_filter_pa_kernel(tc, Mij, f_weights, W1_rel, node_bias, W2, b2, out):
         w1_grp = {}
 
         def regroup_w1(g, half):
-            cols = slice(half * BLOCK, (half + 1) * BLOCK)
-            w1_grp[(g, half)] = stage.tile([P, BLOCK, PACK], BF16, name="w1_grp", tag="w1_grp", align_bytes=64)
-            regroup(w1_grp[(g, half)][:], w1_raw[:, g].rearrange("p u e n -> p (u e) n")[:, :, cols])
+            w1_grp[(g, half)] = stage.tile([P, HALF, PACK], BF16, name="w1_grp", tag="w1_grp", align_bytes=64)
+            regroup(w1_grp[(g, half)][:], w1_raw[half][:, g].rearrange("p u e n -> p (u e) n"))
 
         def quantise_w1(g, half):
-            cols = slice(half * BLOCK, (half + 1) * BLOCK)
+            cols = slice(half * HALF, (half + 1) * HALF)
             quantise(
                 w1_codes[:, g, cols], w1_scales[:, g, cols], w1_grp[(g, half)][:].rearrange("p n j -> p (n j)")
             )
@@ -208,16 +220,16 @@ def tile_filter_pa_kernel(tc, Mij, f_weights, W1_rel, node_bias, W2, b2, out):
                 )
             excess = stage.tile([P, len(tiles)], F32, name="excess", tag="excess")
             nc.scalar.activation(out=excess[:], in_=sumsq[:], func=ACT.Relu, bias=minus_one[:], scale=1.0)
-            norm[(b, tiles[0])] = stage.tile([P, len(tiles)], F32, name="norm", tag="norm")
-            nc.scalar.activation(out=norm[(b, tiles[0])][:], in_=excess[:], func=ACT.Sqrt, bias=plus_one[:], scale=1.0)
+            factor[(b, tiles[0])] = stage.tile([P, len(tiles)], F32, name="factor", tag="factor")
+            nc.scalar.activation(
+                out=factor[(b, tiles[0])][:], in_=excess[:], func=ACT.Abs_reciprocal_sqrt, bias=plus_one[:], scale=1.0
+            )
 
         def scale_and_store(b, tiles):
             shape = [P, len(tiles), D_HET]
-            inverse = stage.tile([P, len(tiles)], F32, name="inverse", tag="inverse")
-            nc.vector.reciprocal(out=inverse[:], in_=norm[(b, tiles[0])][:])
             result = stage.tile(shape, F32, name="result", tag="result")
             nc.vector.tensor_tensor(
-                out=result[:], in0=msg[(b, tiles[0])][:], in1=inverse[:].unsqueeze(2).to_broadcast(shape), op=ALU.mult
+                out=result[:], in0=msg[(b, tiles[0])][:], in1=factor[(b, tiles[0])][:].unsqueeze(2).to_broadcast(shape), op=ALU.mult
             )
             nc.sync.dma_start(out=out_view[b][:, tiles[0] : tiles[-1] + 1, :], in_=result[:])
 

@@ -56,12 +56,13 @@ def tile_filter_pa_kernel(tc, Mij, f_weights, W1_rel, node_bias, W2, b2, out):
                     in_=w1_view[e][:, :, half * HALF : (half + 1) * HALF],
                 )
 
-        def load_mij(b):
-            nc.sync.dma_start(out=mij_raw[b][:], in_=mij_view[b])
+        def load_mij(b, first=0, last=TILES):
+            nc.sync.dma_start(out=mij_raw[b][:, first:last, :], in_=mij_view[b][:, first:last, :])
 
         with tc.manual_schedule(engines={mybir.EngineType.SP}):
+            load_mij(0, 0, TILES // 2)
             load_w1(0)
-            load_mij(0)
+            load_mij(0, TILES // 2, TILES)
             load_mij(1)
             load_w1(1)
             for b in range(2, N_BLOCKS):
@@ -260,6 +261,7 @@ def tile_filter_pa_kernel(tc, Mij, f_weights, W1_rel, node_bias, W2, b2, out):
         prepare_w2()
         for b in range(1, BLOCKS_AHEAD + 1):
             prepare_mij(b)
+        waiting = []
         for b in range(N_BLOCKS):
             n_parts = LAST_PARTS if b == N_BLOCKS - 1 else 1
             size = TILES // n_parts
@@ -273,6 +275,13 @@ def tile_filter_pa_kernel(tc, Mij, f_weights, W1_rel, node_bias, W2, b2, out):
                     quantise_h(b, g2, tiles)
             if b + BLOCKS_AHEAD + 1 < N_BLOCKS:
                 prepare_mij(b + BLOCKS_AHEAD + 1)
-            for step in (second_layer, message, clamped_norm, scale_and_store):
+            for step in (second_layer, message):
                 for tiles in parts:
                     step(b, tiles)
+            for step in (clamped_norm, scale_and_store):
+                for tiles in waiting:
+                    step(b - 1, tiles)
+            waiting = parts
+        for step in (clamped_norm, scale_and_store):
+            for tiles in waiting:
+                step(N_BLOCKS - 1, tiles)

@@ -22,6 +22,7 @@ HALF = D_HID // 2
 HID_TILES = D_HID // P
 BLOCKS_AHEAD = 1
 LAST_PARTS = 2
+SCALAR_COLS = 192
 RUN = 4
 
 FLOPS = 2 * EDGES * D_REL * D_HID + 2 * EDGES * D_HID * D_HET
@@ -134,7 +135,14 @@ def tile_filter_pa_kernel(tc, Mij, f_weights, W1_rel, node_bias, W2, b2, out):
 
         def regroup_w1(g, half):
             w1_grp[(g, half)] = stage.tile([P, HALF, PACK], BF16, name="w1_grp", tag="w1_grp", align_bytes=64)
-            regroup(w1_grp[(g, half)][:], w1_raw[half][:, g].rearrange("p u e n -> p (u e) n"))
+            raw = w1_raw[half][:, g].rearrange("p u e n -> p (u e) n")
+            mine = HALF - SCALAR_COLS if half == 0 else HALF
+            regroup(w1_grp[(g, half)][:, :mine, :], raw[:, :, :mine])
+            if mine < HALF:
+                nc.scalar.copy(
+                    out=w1_grp[(g, half)][:, mine:, :].rearrange("p (c i) j -> p c j i", i=RUN),
+                    in_=raw[:, :, mine:].rearrange("p j (c i) -> p c j i", i=RUN),
+                )
 
         def quantise_w1(g, half):
             cols = slice(half * HALF, (half + 1) * HALF)
@@ -169,7 +177,13 @@ def tile_filter_pa_kernel(tc, Mij, f_weights, W1_rel, node_bias, W2, b2, out):
             if tiles[0] == 0:
                 h_grp[(b, g2)] = stage.tile([P, BLOCK, PACK], BF16, name="h_grp", tag="h_grp", align_bytes=64)
             cols = edge_cols(tiles)
-            regroup(h_grp[(b, g2)][:, cols, :], h_planes[(b, g2)][:, :, cols])
+            if b == N_BLOCKS - 1 and g2 == PASSES - 1 and tiles[0] > 0:
+                nc.scalar.copy(
+                    out=h_grp[(b, g2)][:, cols, :].rearrange("p (c i) j -> p c j i", i=RUN),
+                    in_=h_planes[(b, g2)][:, :, cols].rearrange("p j (c i) -> p c j i", i=RUN),
+                )
+            else:
+                regroup(h_grp[(b, g2)][:, cols, :], h_planes[(b, g2)][:, :, cols])
 
         def quantise_h(b, g2, tiles):
             if g2 == 0 and tiles[0] == 0:
@@ -229,9 +243,21 @@ def tile_filter_pa_kernel(tc, Mij, f_weights, W1_rel, node_bias, W2, b2, out):
         def scale_and_store(b, tiles):
             shape = [P, len(tiles), D_HET]
             result = stage.tile(shape, F32, name="result", tag="result")
-            nc.vector.tensor_tensor(
-                out=result[:], in0=msg[(b, tiles[0])][:], in1=factor[(b, tiles[0])][:].unsqueeze(2).to_broadcast(shape), op=ALU.mult
-            )
+            if b == N_BLOCKS - 2:
+                for i in range(len(tiles)):
+                    nc.scalar.activation(
+                        out=result[:, i, :],
+                        in_=msg[(b, tiles[0])][:, i, :],
+                        func=ACT.Copy,
+                        scale=factor[(b, tiles[0])][:, i : i + 1],
+                    )
+            else:
+                nc.vector.tensor_tensor(
+                    out=result[:],
+                    in0=msg[(b, tiles[0])][:],
+                    in1=factor[(b, tiles[0])][:].unsqueeze(2).to_broadcast(shape),
+                    op=ALU.mult,
+                )
             nc.sync.dma_start(out=out_view[b][:, tiles[0] : tiles[-1] + 1, :], in_=result[:])
 
         def prepare_w2():
@@ -273,11 +299,21 @@ def tile_filter_pa_kernel(tc, Mij, f_weights, W1_rel, node_bias, W2, b2, out):
                     regroup_h(b, g2, tiles)
                 for tiles in parts:
                     quantise_h(b, g2, tiles)
-            if b + BLOCKS_AHEAD + 1 < N_BLOCKS:
-                prepare_mij(b + BLOCKS_AHEAD + 1)
-            for step in (second_layer, message):
-                for tiles in parts:
-                    step(b, tiles)
+                if g2 == 0 and b + BLOCKS_AHEAD + 1 < N_BLOCKS:
+                    prepare_mij(b + BLOCKS_AHEAD + 1)
+            for tiles in parts:
+                second_layer(b, tiles)
+            if b == N_BLOCKS - 2:
+                for step in (clamped_norm, scale_and_store):
+                    for tiles in waiting:
+                        step(b - 1, tiles)
+                waiting = parts
+                continue
+            if b == N_BLOCKS - 1:
+                for tiles in waiting:
+                    message(b - 1, tiles)
+            for tiles in parts:
+                message(b, tiles)
             for step in (clamped_norm, scale_and_store):
                 for tiles in waiting:
                     step(b - 1, tiles)

@@ -95,7 +95,7 @@ def tile_filter_pa_kernel(tc, Mij, f_weights, W1_rel, node_bias, W2, b2, out):
         w2_scales = const.tile([P, PASSES, D_HET], U8, align_bytes=64)
         mij_grp, mij_codes, mij_scales = {}, {}, {}
         h_planes, h_grp, h_codes, h_scales = {}, {}, {}, {}
-        o_bank, msg, factor = {}, {}, {}
+        o_bank, biased, msg, factor = {}, {}, {}, {}
 
         def regroup(dst, src):
             nc.vector.tensor_copy(
@@ -212,15 +212,23 @@ def tile_filter_pa_kernel(tc, Mij, f_weights, W1_rel, node_bias, W2, b2, out):
                         stop=(g2 == PASSES - 1),
                     )
 
-        def message(b, tiles):
+        def add_b2(b, tiles):
             shape = [P, len(tiles), D_HET]
-            biased = stage.tile(shape, F32, name="biased", tag="biased")
+            biased[(b, tiles[0])] = stage.tile(shape, F32, name="biased", tag="biased")
             nc.vector.tensor_tensor(
-                out=biased[:], in0=o_bank[(b, tiles[0])][:], in1=b2_all[:].unsqueeze(1).to_broadcast(shape), op=ALU.add
+                out=biased[(b, tiles[0])][:],
+                in0=o_bank[(b, tiles[0])][:],
+                in1=b2_all[:].unsqueeze(1).to_broadcast(shape),
+                op=ALU.add,
             )
-            msg[(b, tiles[0])] = stage.tile(shape, F32, name="msg", tag="msg")
+
+        def times_f_weights(b, tiles):
+            msg[(b, tiles[0])] = stage.tile([P, len(tiles), D_HET], F32, name="msg", tag="msg")
             nc.vector.tensor_tensor(
-                out=msg[(b, tiles[0])][:], in0=biased[:], in1=fw_sb[:, b, tiles[0] : tiles[-1] + 1, :], op=ALU.mult
+                out=msg[(b, tiles[0])][:],
+                in0=biased[(b, tiles[0])][:],
+                in1=fw_sb[:, b, tiles[0] : tiles[-1] + 1, :],
+                op=ALU.mult,
             )
 
         def clamped_norm(b, tiles):
@@ -287,37 +295,42 @@ def tile_filter_pa_kernel(tc, Mij, f_weights, W1_rel, node_bias, W2, b2, out):
         prepare_w2()
         for b in range(1, BLOCKS_AHEAD + 1):
             prepare_mij(b)
-        waiting = []
+        whole = [list(range(TILES))]
+        size = TILES // LAST_PARTS
+        halves = [list(range(i * size, (i + 1) * size)) for i in range(LAST_PARTS)]
         for b in range(N_BLOCKS):
-            n_parts = LAST_PARTS if b == N_BLOCKS - 1 else 1
-            size = TILES // n_parts
-            parts = [list(range(i * size, (i + 1) * size)) for i in range(n_parts)]
+            last = b == N_BLOCKS - 1
+            parts = halves if last else whole
+            message_before = b > 0 and not last
+            prepare_next = b + BLOCKS_AHEAD + 1 < N_BLOCKS
             for g2 in range(PASSES):
                 for t in range(PACK):
                     first_layer(b, g2 * PACK + t)
                 for tiles in parts:
                     regroup_h(b, g2, tiles)
+                if g2 == 0 and message_before:
+                    add_b2(b - 1, whole[0])
+                if g2 == 1 and prepare_next:
+                    quantise_mij(b + BLOCKS_AHEAD + 1)
                 for tiles in parts:
                     quantise_h(b, g2, tiles)
-                if g2 == 0 and b + BLOCKS_AHEAD + 1 < N_BLOCKS:
-                    prepare_mij(b + BLOCKS_AHEAD + 1)
+                if g2 == 0 and message_before:
+                    times_f_weights(b - 1, whole[0])
+                if g2 == 0 and prepare_next:
+                    transpose_pair(2 * (b + BLOCKS_AHEAD + 1))
+                    transpose_pair(2 * (b + BLOCKS_AHEAD + 1) + 1)
             for tiles in parts:
                 second_layer(b, tiles)
-            if b == N_BLOCKS - 2:
-                for step in (clamped_norm, scale_and_store):
-                    for tiles in waiting:
-                        step(b - 1, tiles)
-                waiting = parts
-                continue
-            if b == N_BLOCKS - 1:
-                for tiles in waiting:
-                    message(b - 1, tiles)
-            for tiles in parts:
-                message(b, tiles)
+            if message_before:
+                clamped_norm(b - 1, whole[0])
+                scale_and_store(b - 1, whole[0])
+        add_b2(N_BLOCKS - 2, whole[0])
+        add_b2(N_BLOCKS - 1, halves[0])
+        times_f_weights(N_BLOCKS - 2, whole[0])
+        add_b2(N_BLOCKS - 1, halves[1])
+        for tiles in halves:
+            times_f_weights(N_BLOCKS - 1, tiles)
+        for b, parts in ((N_BLOCKS - 2, whole), (N_BLOCKS - 1, halves)):
             for step in (clamped_norm, scale_and_store):
-                for tiles in waiting:
-                    step(b - 1, tiles)
-            waiting = parts
-        for step in (clamped_norm, scale_and_store):
-            for tiles in waiting:
-                step(N_BLOCKS - 1, tiles)
+                for tiles in parts:
+                    step(b, tiles)

@@ -23,6 +23,7 @@ HID_TILES = D_HID // P
 BLOCKS_AHEAD = 1
 LAST_PARTS = 2
 SCALAR_COLS = 192
+SCALED_BY_SCALAR = N_BLOCKS - 2
 RUN = 4
 
 FLOPS = 2 * EDGES * D_REL * D_HID + 2 * EDGES * D_HID * D_HET
@@ -82,6 +83,8 @@ def tile_filter_pa_kernel(tc, Mij, f_weights, W1_rel, node_bias, W2, b2, out):
         nc.vector.memset(plus_one[:], 1.0)
         minus_one = const.tile([P, 1], F32)
         nc.vector.memset(minus_one[:], -1.0)
+        tiny = const.tile([P, 1], F32)
+        nc.vector.memset(tiny[:], 2.0**-80)
         warm = const.tile([P, 1], F32)
         nc.scalar.activation(out=warm[:], in_=plus_one[:], func=ACT.Abs_reciprocal_sqrt)
 
@@ -241,17 +244,26 @@ def tile_filter_pa_kernel(tc, Mij, f_weights, W1_rel, node_bias, W2, b2, out):
                     func=ACT.Square,
                     accum_out=sumsq[:, i : i + 1],
                 )
-            excess = stage.tile([P, len(tiles)], F32, name="excess", tag="excess")
-            nc.scalar.activation(out=excess[:], in_=sumsq[:], func=ACT.Relu, bias=minus_one[:], scale=1.0)
             factor[(b, tiles[0])] = stage.tile([P, len(tiles)], F32, name="factor", tag="factor")
-            nc.scalar.activation(
-                out=factor[(b, tiles[0])][:], in_=excess[:], func=ACT.Abs_reciprocal_sqrt, bias=plus_one[:], scale=1.0
-            )
+            if b == SCALED_BY_SCALAR:
+                excess = stage.tile([P, len(tiles)], F32, name="excess", tag="excess")
+                nc.scalar.activation(out=excess[:], in_=sumsq[:], func=ACT.Relu, bias=minus_one[:], scale=1.0)
+                nc.scalar.activation(
+                    out=factor[(b, tiles[0])][:],
+                    in_=excess[:],
+                    func=ACT.Abs_reciprocal_sqrt,
+                    bias=plus_one[:],
+                    scale=1.0,
+                )
+            else:
+                nc.scalar.activation(
+                    out=factor[(b, tiles[0])][:], in_=sumsq[:], func=ACT.Abs_reciprocal_sqrt, bias=tiny[:], scale=1.0
+                )
 
         def scale_and_store(b, tiles):
             shape = [P, len(tiles), D_HET]
             result = stage.tile(shape, F32, name="result", tag="result")
-            if b == N_BLOCKS - 2:
+            if b == SCALED_BY_SCALAR:
                 for i in range(len(tiles)):
                     nc.scalar.activation(
                         out=result[:, i, :],
@@ -260,11 +272,13 @@ def tile_filter_pa_kernel(tc, Mij, f_weights, W1_rel, node_bias, W2, b2, out):
                         scale=factor[(b, tiles[0])][:, i : i + 1],
                     )
             else:
-                nc.vector.tensor_tensor(
+                nc.vector.scalar_tensor_tensor(
                     out=result[:],
-                    in0=msg[(b, tiles[0])][:],
-                    in1=factor[(b, tiles[0])][:].unsqueeze(2).to_broadcast(shape),
-                    op=ALU.mult,
+                    in0=factor[(b, tiles[0])][:].unsqueeze(2).to_broadcast(shape),
+                    scalar=1.0,
+                    in1=msg[(b, tiles[0])][:],
+                    op0=ALU.min,
+                    op1=ALU.mult,
                 )
             nc.sync.dma_start(out=out_view[b][:, tiles[0] : tiles[-1] + 1, :], in_=result[:])
 

@@ -41,7 +41,7 @@ def tile_filter_pa_kernel(tc, Mij, f_weights, W1_rel, node_bias, W2, b2, out):
 
     with ExitStack() as ctx:
         const = ctx.enter_context(tc.tile_pool(name="const", bufs=1))
-        stage = ctx.enter_context(tc.tile_pool(name="stage", bufs=3))
+        stage = ctx.enter_context(tc.tile_pool(name="stage", bufs=4))
         psum = ctx.enter_context(tc.psum_pool(name="psum", bufs=8))
 
         mij_raw = [

from contextlib import ExitStack

import concourse.mybir as mybir
from concourse.masks import make_identity

F32 = mybir.dt.float32
BF16 = mybir.dt.bfloat16
U32 = mybir.dt.uint32
U8 = mybir.dt.uint8
FP8X4 = mybir.dt.float8_e4m3fn_x4
ACT = mybir.ActivationFunctionType
ALU = mybir.AluOpType

P = 128
PACK = 4
PASSES = 2
EDGES, D_REL, D_HID, D_HET = 2048, 1024, 1024, 128
BLOCK = 512
N_BLOCKS = EDGES // BLOCK
TILES = BLOCK // P
HALF = D_HID // 2
HID_TILES = D_HID // P
BLOCKS_AHEAD = 1
LAST_PARTS = 2
SCALAR_COLS = 192
SCALED_BY_SCALAR = N_BLOCKS - 2
RUN = 4

FLOPS = 2 * EDGES * D_REL * D_HID + 2 * EDGES * D_HID * D_HET


def tile_filter_pa_kernel(tc, Mij, f_weights, W1_rel, node_bias, W2, b2, out):
    nc = tc.nc

    mij_view = Mij.rearrange("(b p t) k -> b p t k", b=N_BLOCKS, p=P, t=TILES)
    fw_view = f_weights.rearrange("(b p t) h -> p b t h", b=N_BLOCKS, p=P, t=TILES)
    out_view = out.rearrange("(b p t) h -> b p t h", b=N_BLOCKS, p=P, t=TILES)
    w1_view = W1_rel.rearrange("(c p e) n -> e p c n", c=2 * PASSES, p=P, e=2)
    w2_view = W2.rearrange("(g t p) n -> p g t n", g=PASSES, t=PACK, p=P)
    nb_view = node_bias.rearrange("(r c) -> r c", c=P)

    with ExitStack() as ctx:
        const = ctx.enter_context(tc.tile_pool(name="const", bufs=1))
        stage = ctx.enter_context(tc.tile_pool(name="stage", bufs=4))
        psum = ctx.enter_context(tc.psum_pool(name="psum", bufs=8))

        mij_raw = [
            const.tile([P, TILES, D_REL], BF16, name="mij_raw%d" % b) for b in range(N_BLOCKS)
        ]
        w1_raw = [const.tile([P, PASSES, 2, 2, HALF], BF16, name="w1_raw%d" % half) for half in range(2)]
        nb_rows = const.tile([P, P], BF16)
        nc.vector.memset(nb_rows[:], 0.0)
        nc.sync.dma_start(out=nb_rows[0:HID_TILES, :], in_=nb_view)
        def load_w1(half):
            for e in range(2):
                nc.sync.dma_start(
                    out=w1_raw[half][:, :, :, e, :].rearrange("p g u n -> p (g u) n"),
                    in_=w1_view[e][:, :, half * HALF : (half + 1) * HALF],
                )

        def load_mij(b, first=0, last=TILES):
            nc.sync.dma_start(out=mij_raw[b][:, first:last, :], in_=mij_view[b][:, first:last, :])

        with tc.manual_schedule(engines={mybir.EngineType.SP}):
            load_mij(0, 0, TILES // 2)
            load_w1(0)
            load_mij(0, TILES // 2, TILES)
            load_mij(1)
            load_w1(1)
            for b in range(2, N_BLOCKS):
                load_mij(b)

        w2_raw = const.tile([P, PASSES, PACK, D_HET], BF16)
        nc.sync.dma_start(out=w2_raw[:], in_=w2_view)
        fw_sb = const.tile([P, N_BLOCKS, TILES, D_HET], BF16)
        nc.sync.dma_start(out=fw_sb[:], in_=fw_view)
        b2_all = const.tile([P, D_HET], BF16)
        nc.sync.dma_start(out=b2_all[:], in_=b2.partition_broadcast(P))

        ident = const.tile([P, P], F32)
        make_identity(nc, ident[:])
        plus_one = const.tile([P, 1], F32)
        nc.vector.memset(plus_one[:], 1.0)
        minus_one = const.tile([P, 1], F32)
        nc.vector.memset(minus_one[:], -1.0)
        tiny = const.tile([P, 1], F32)
        nc.vector.memset(tiny[:], 2.0**-80)
        warm = const.tile([P, 1], F32)
        nc.scalar.activation(out=warm[:], in_=plus_one[:], func=ACT.Abs_reciprocal_sqrt)

        nb_f32 = const.tile([P, P], F32)
        nc.vector.tensor_copy(out=nb_f32[:], in_=nb_rows[:])
        nb_col = const.tile([P, HID_TILES], F32)

        w1_codes = const.tile([P, PASSES, D_HID], U32, align_bytes=64)
        w1_scales = const.tile([P, PASSES, D_HID], U8, align_bytes=64)
        w2_codes = const.tile([P, PASSES, D_HET], U32, align_bytes=64)
        w2_scales = const.tile([P, PASSES, D_HET], U8, align_bytes=64)
        mij_grp, mij_codes, mij_scales = {}, {}, {}
        h_planes, h_grp, h_codes, h_scales = {}, {}, {}, {}
        o_bank, biased, msg, factor = {}, {}, {}, {}

        def regroup(dst, src):
            nc.vector.tensor_copy(
                out=dst.rearrange("p (c i) j -> p c j i", i=RUN),
                in_=src.rearrange("p j (c i) -> p c j i", i=RUN),
            )

        def quantise(codes, scales, grouped):
            nc.vector.quantize_mx(out=codes.bitcast(FP8X4), scales=scales, in_=grouped)

        def transpose_pair(pair):
            b, half = divmod(pair, 2)
            if half == 0:
                mij_grp[b] = stage.tile([P, PASSES, BLOCK, 2], F32, name="mij_grp", tag="mij_grp", align_bytes=64)
            for t in (2 * half, 2 * half + 1):
                words = mij_raw[b][:, t, :].bitcast(F32)
                bank = psum.tile([P, PASSES, 2, P], F32, name="tr_bank", tag="bank")
                for g in range(PASSES):
                    for u in range(2):
                        first = (2 * g + u) * P
                        nc.tensor.transpose(bank[:, g, u, :], words[:, first : first + P], ident[:])
                nc.scalar.copy(
                    out=mij_grp[b][:, :, t * P : (t + 1) * P, :],
                    in_=bank[:].rearrange("p g u e -> p g e u"),
                )

        def quantise_mij(b):
            mij_codes[b] = stage.tile([P, PASSES, BLOCK], U32, name="mij_codes", tag="mij_codes", align_bytes=64)
            mij_scales[b] = stage.tile([P, PASSES, BLOCK], U8, name="mij_scales", tag="mij_scales", align_bytes=64)
            quantise(
                mij_codes[b][:].rearrange("p g e -> p (g e)"),
                mij_scales[b][:].rearrange("p g e -> p (g e)"),
                mij_grp[b][:].rearrange("p g e u -> p (g e u)").bitcast(BF16),
            )

        w1_grp = {}

        def regroup_w1(g, half):
            w1_grp[(g, half)] = stage.tile([P, HALF, PACK], BF16, name="w1_grp", tag="w1_grp", align_bytes=64)
            raw = w1_raw[half][:, g].rearrange("p u e n -> p (u e) n")
            mine = HALF - SCALAR_COLS if half == 0 else HALF
            regroup(w1_grp[(g, half)][:, :mine, :], raw[:, :, :mine])
            if mine < HALF:
                nc.scalar.copy(
                    out=w1_grp[(g, half)][:, mine:, :].rearrange("p (c i) j -> p c j i", i=RUN),
                    in_=raw[:, :, mine:].rearrange("p j (c i) -> p c j i", i=RUN),
                )

        def quantise_w1(g, half):
            cols = slice(half * HALF, (half + 1) * HALF)
            quantise(
                w1_codes[:, g, cols], w1_scales[:, g, cols], w1_grp[(g, half)][:].rearrange("p n j -> p (n j)")
            )

        def first_layer(b, m):
            g2, t = divmod(m, PACK)
            if t == 0:
                h_planes[(b, g2)] = stage.tile([P, PACK, BLOCK], BF16, name="h_planes", tag="h_planes")
            cols = slice(m * P, (m + 1) * P)
            bank = psum.tile([P, BLOCK], F32, name="h_bank", tag="bank")
            for g in range(PASSES):
                nc.tensor.matmul_mx(
                    out=bank[:],
                    lhsT=w1_codes[:, g, cols].bitcast(FP8X4),
                    lhsT_scale=w1_scales[:, g, cols],
                    rhs=mij_codes[b][:, g, :].bitcast(FP8X4),
                    rhs_scale=mij_scales[b][:, g, :],
                    start=(g == 0),
                    stop=(g == PASSES - 1),
                )
            nc.scalar.activation(
                out=h_planes[(b, g2)][:, t, :], in_=bank[:], func=ACT.Relu, bias=nb_col[:, m : m + 1], scale=1.0
            )

        def edge_cols(tiles):
            return slice(tiles[0] * P, (tiles[-1] + 1) * P)

        def regroup_h(b, g2, tiles):
            if tiles[0] == 0:
                h_grp[(b, g2)] = stage.tile([P, BLOCK, PACK], BF16, name="h_grp", tag="h_grp", align_bytes=64)
            cols = edge_cols(tiles)
            if b == N_BLOCKS - 1 and g2 == PASSES - 1 and tiles[0] > 0:
                nc.scalar.copy(
                    out=h_grp[(b, g2)][:, cols, :].rearrange("p (c i) j -> p c j i", i=RUN),
                    in_=h_planes[(b, g2)][:, :, cols].rearrange("p j (c i) -> p c j i", i=RUN),
                )
            else:
                regroup(h_grp[(b, g2)][:, cols, :], h_planes[(b, g2)][:, :, cols])

        def quantise_h(b, g2, tiles):
            if g2 == 0 and tiles[0] == 0:
                h_codes[b] = stage.tile([P, PASSES, BLOCK], U32, name="h_codes", tag="h_codes", align_bytes=64)
                h_scales[b] = stage.tile([P, PASSES, BLOCK], U8, name="h_scales", tag="h_scales", align_bytes=64)
            cols = edge_cols(tiles)
            quantise(
                h_codes[b][:, g2, cols],
                h_scales[b][:, g2, cols],
                h_grp[(b, g2)][:, cols, :].rearrange("p e j -> p (e j)"),
            )

        def second_layer(b, tiles):
            bank = psum.tile([P, len(tiles), D_HET], F32, name="o_bank", tag="bank")
            o_bank[(b, tiles[0])] = bank
            for i, t in enumerate(tiles):
                cols = slice(t * P, (t + 1) * P)
                for g2 in range(PASSES):
                    nc.tensor.matmul_mx(
                        out=bank[:, i, :],
                        lhsT=h_codes[b][:, g2, cols].bitcast(FP8X4),
                        lhsT_scale=h_scales[b][:, g2, cols],
                        rhs=w2_codes[:, g2, :].bitcast(FP8X4),
                        rhs_scale=w2_scales[:, g2, :],
                        start=(g2 == 0),
                        stop=(g2 == PASSES - 1),
                    )

        def add_b2(b, tiles):
            shape = [P, len(tiles), D_HET]
            biased[(b, tiles[0])] = stage.tile(shape, F32, name="biased", tag="biased")
            nc.vector.tensor_tensor(
                out=biased[(b, tiles[0])][:],
                in0=o_bank[(b, tiles[0])][:],
                in1=b2_all[:].unsqueeze(1).to_broadcast(shape),
                op=ALU.add,
            )

        def times_f_weights(b, tiles):
            msg[(b, tiles[0])] = stage.tile([P, len(tiles), D_HET], F32, name="msg", tag="msg")
            nc.vector.tensor_tensor(
                out=msg[(b, tiles[0])][:],
                in0=biased[(b, tiles[0])][:],
                in1=fw_sb[:, b, tiles[0] : tiles[-1] + 1, :],
                op=ALU.mult,
            )

        def clamped_norm(b, tiles):
            squares = stage.tile([P, len(tiles), D_HET], F32, name="squares", tag="squares")
            sumsq = stage.tile([P, len(tiles)], F32, name="sumsq", tag="sumsq")
            for i in range(len(tiles)):
                nc.scalar.activation(
                    out=squares[:, i, :],
                    in_=msg[(b, tiles[0])][:, i, :],
                    func=ACT.Square,
                    accum_out=sumsq[:, i : i + 1],
                )
            factor[(b, tiles[0])] = stage.tile([P, len(tiles)], F32, name="factor", tag="factor")
            if b == SCALED_BY_SCALAR:
                excess = stage.tile([P, len(tiles)], F32, name="excess", tag="excess")
                nc.scalar.activation(out=excess[:], in_=sumsq[:], func=ACT.Relu, bias=minus_one[:], scale=1.0)
                nc.scalar.activation(
                    out=factor[(b, tiles[0])][:],
                    in_=excess[:],
                    func=ACT.Abs_reciprocal_sqrt,
                    bias=plus_one[:],
                    scale=1.0,
                )
            else:
                nc.scalar.activation(
                    out=factor[(b, tiles[0])][:], in_=sumsq[:], func=ACT.Abs_reciprocal_sqrt, bias=tiny[:], scale=1.0
                )

        def scale_and_store(b, tiles):
            shape = [P, len(tiles), D_HET]
            result = stage.tile(shape, F32, name="result", tag="result")
            if b == SCALED_BY_SCALAR:
                for i in range(len(tiles)):
                    nc.scalar.activation(
                        out=result[:, i, :],
                        in_=msg[(b, tiles[0])][:, i, :],
                        func=ACT.Copy,
                        scale=factor[(b, tiles[0])][:, i : i + 1],
                    )
            else:
                nc.vector.scalar_tensor_tensor(
                    out=result[:],
                    in0=factor[(b, tiles[0])][:].unsqueeze(2).to_broadcast(shape),
                    scalar=1.0,
                    in1=msg[(b, tiles[0])][:],
                    op0=ALU.min,
                    op1=ALU.mult,
                )
            nc.sync.dma_start(out=out_view[b][:, tiles[0] : tiles[-1] + 1, :], in_=result[:])

        def prepare_w2():
            w2_grp = const.tile([P, PASSES, D_HET, PACK], BF16, align_bytes=64)
            for g2 in range(PASSES):
                regroup(w2_grp[:, g2], w2_raw[:, g2])
            quantise(
                w2_codes[:].rearrange("p g n -> p (g n)"),
                w2_scales[:].rearrange("p g n -> p (g n)"),
                w2_grp[:].rearrange("p g n j -> p (g n j)"),
            )

        def prepare_mij(b):
            transpose_pair(2 * b)
            transpose_pair(2 * b + 1)
            quantise_mij(b)

        nb_bank = psum.tile([P, P], F32, name="nb_bank", tag="bank")
        nc.tensor.transpose(nb_bank[:], nb_f32[:], ident[:])
        nc.vector.tensor_copy(out=nb_col[:], in_=nb_bank[:, 0:HID_TILES])
        prepare_mij(0)
        for half in range(2):
            for g in range(PASSES):
                regroup_w1(g, half)
            for g in range(PASSES):
                quantise_w1(g, half)
        prepare_w2()
        for b in range(1, BLOCKS_AHEAD + 1):
            prepare_mij(b)
        whole = [list(range(TILES))]
        size = TILES // LAST_PARTS
        halves = [list(range(i * size, (i + 1) * size)) for i in range(LAST_PARTS)]
        for b in range(N_BLOCKS):
            last = b == N_BLOCKS - 1
            parts = halves if last else whole
            message_before = b > 0 and not last
            prepare_next = b + BLOCKS_AHEAD + 1 < N_BLOCKS
            for g2 in range(PASSES):
                for t in range(PACK):
                    first_layer(b, g2 * PACK + t)
                for tiles in parts:
                    regroup_h(b, g2, tiles)
                if g2 == 0 and message_before:
                    add_b2(b - 1, whole[0])
                if g2 == 1 and prepare_next:
                    quantise_mij(b + BLOCKS_AHEAD + 1)
                for tiles in parts:
                    quantise_h(b, g2, tiles)
                if g2 == 0 and message_before:
                    times_f_weights(b - 1, whole[0])
                if g2 == 0 and prepare_next:
                    transpose_pair(2 * (b + BLOCKS_AHEAD + 1))
                    transpose_pair(2 * (b + BLOCKS_AHEAD + 1) + 1)
            for tiles in parts:
                second_layer(b, tiles)
            if message_before:
                clamped_norm(b - 1, whole[0])
                scale_and_store(b - 1, whole[0])
        add_b2(N_BLOCKS - 2, whole[0])
        add_b2(N_BLOCKS - 1, halves[0])
        times_f_weights(N_BLOCKS - 2, whole[0])
        add_b2(N_BLOCKS - 1, halves[1])
        for tiles in halves:
            times_f_weights(N_BLOCKS - 1, tiles)
        for b, parts in ((N_BLOCKS - 2, whole), (N_BLOCKS - 1, halves)):
            for step in (clamped_norm, scale_and_store):
                for tiles in parts:
                    step(b, tiles)
